import numpy as np
import ml_dtypes


def mxq(x, axis, fmt="e4m3"):
    dtype, down = {"e4m3": (ml_dtypes.float8_e4m3fn, 7), "e5m2": (ml_dtypes.float8_e5m2, 14)}[fmt]
    v = np.moveaxis(np.asarray(x, np.float32).astype(ml_dtypes.bfloat16).astype(np.float64), axis, -1)
    blocks = v.reshape(v.shape[:-1] + (-1, 32))
    amax = np.abs(blocks).max(-1, keepdims=True)
    byte = np.maximum(np.where(amax > 0, np.frexp(amax)[1] - 1 + 127, 0) - down, 1)
    scale = np.exp2(byte - 127.0)
    codes = (blocks / scale).astype(np.float32).astype(dtype).astype(np.float64)
    return np.moveaxis((codes * scale).reshape(v.shape), -1, axis)


WIDE = False


def mx_kscale(k):
    if not WIDE:
        return np.ones(k)
    levels = np.array([10, -10, 5, -5, 0])
    a = np.random.permutation(np.resize(levels, k // 512 * 4)).reshape(k // 512, 4)
    idx = np.arange(k)
    return np.exp2(a[idx // 512, idx % 128 // 32])


BF16 = ml_dtypes.bfloat16


def bf(x):
    return np.asarray(x, np.float32).astype(BF16)


def f64(x):
    return np.asarray(x).astype(np.float64)


NS, NI, T = 1024, 512, 1025
NA = NS + NI


def setup_inputs():
    s = mx_kscale(NA)
    r = s[:NS]
    A = np.random.standard_normal((NS, NS)) / np.sqrt(NA)
    B = np.random.standard_normal((NS, NI)) / np.sqrt(NA)
    x0 = np.random.standard_normal(NS) * 3.0
    V = np.random.standard_normal((T, NA))
    V[0, :NS] *= 3.0
    return {"A": bf(A * r[:, None] / s[None, :NS]), "B": bf(B * r[:, None] / s[None, NS:]), "x0": bf(x0 * r),
            "net_input": bf((V * s[None, :]).reshape(-1)), "T": T}


def reference(A, B, x0, net_input, T):
    n_state = A.shape[0]
    n_all = n_state + B.shape[1]
    AB = np.concatenate([f64(A), f64(B)], axis=1)
    V = f64(net_input).reshape(T, n_all)
    out0 = V[0, :n_state] - f64(x0)
    prop = mxq(V[:-1], 1, "e4m3") @ mxq(AB, 1, "e4m3").T
    out_rest = prop - V[1:, :n_state]
    return np.concatenate([out0, out_rest.reshape(-1)])

@@ -1,0 +1,149 @@
+from contextlib import ExitStack
+
+import concourse.mybir as mybir
+from concourse.masks import make_identity
+
+F32 = mybir.dt.float32
+BF16 = mybir.dt.bfloat16
+U32 = mybir.dt.uint32
+U8 = mybir.dt.uint8
+FP8X4 = mybir.dt.float8_e4m3fn_x4
+
+P = 128
+N_STATE = 1024
+N_ALL = 1536
+STEPS = 1024
+PASSES = 3
+WORDS = 2
+SLOTS = STEPS // P
+TILES = N_STATE // P
+PAIR = 2 * P
+N_HALF = 512
+HALVES = N_STATE // N_HALF
+FIRST_P = 16
+
+FLOPS = 2 * STEPS * N_STATE * N_ALL
+
+
+def prepare_pair(nc, banks, ident, raw, pair, grouped, codes, scales):
+    cols = slice(pair * PAIR, (pair + 1) * PAIR)
+    for g in range(PASSES):
+        bank = banks.tile([P, WORDS, PAIR], F32)
+        for t in range(2):
+            row_words = raw[:, 2 * pair + t, :].bitcast(F32)
+            for u in range(WORDS):
+                first = (WORDS * g + u) * P
+                nc.tensor.transpose(
+                    bank[:, u, t * P : (t + 1) * P], row_words[:, first : first + P], ident[:]
+                )
+        nc.scalar.copy(out=grouped[:, g, cols, :], in_=bank[:].rearrange("p u r -> p r u"))
+    for g in range(PASSES):
+        nc.vector.quantize_mx(
+            out=codes[:, g, cols].bitcast(FP8X4),
+            scales=scales[:, g, cols],
+            in_=grouped[:, g, cols, :].rearrange("p r u -> p (r u)").bitcast(BF16),
+        )
+
+
+def tile_constrainnet_kernel(tc, A, B, x0, net_input, T, out):
+    nc = tc.nc
+    assert T == STEPS + 1
+
+    v_rows = net_input[0 : STEPS * N_ALL].rearrange("(p s k) -> p s k", s=SLOTS, k=N_ALL)
+    v_next = net_input[N_ALL : (STEPS + 1) * N_ALL].rearrange("(p s k) -> p s k", s=SLOTS, k=N_ALL)
+    r_next = out[N_STATE : (STEPS + 1) * N_STATE].rearrange("(p s i) -> p s i", s=SLOTS, i=N_STATE)
+    a_rows = A.rearrange("(m p) k -> p m k", p=P)
+    b_rows = B.rearrange("(m p) k -> p m k", p=P)
+
+    with ExitStack() as ctx:
+        keep = ctx.enter_context(tc.tile_pool(name="keep", bufs=1))
+        banks = ctx.enter_context(tc.psum_pool(name="banks", bufs=4))
+        sums = ctx.enter_context(tc.psum_pool(name="sums", bufs=4))
+
+        ident = keep.tile([P, P], F32)
+        make_identity(nc, ident[:])
+
+        ab_raw = keep.tile([P, TILES, N_ALL], BF16)
+        v_raw = keep.tile([P, SLOTS + 1, N_ALL], BF16)
+        ab_grouped = keep.tile([P, PASSES, N_STATE, WORDS], F32, align_bytes=64)
+        v_grouped = keep.tile([P, PASSES, STEPS, WORDS], F32, align_bytes=64)
+        ab_codes = keep.tile([P, PASSES, N_STATE], U32, align_bytes=64)
+        ab_scales = keep.tile([P, PASSES, N_STATE], U8, align_bytes=64)
+        v_codes = keep.tile([P, PASSES, STEPS], U32, align_bytes=64)
+        v_scales = keep.tile([P, PASSES, STEPS], U8, align_bytes=64)
+        r_sb = keep.tile([P, SLOTS, N_STATE], F32)
+        x_first = keep.tile([FIRST_P, N_STATE // FIRST_P], BF16)
+        x_given = keep.tile([FIRST_P, N_STATE // FIRST_P], BF16)
+        r_first = keep.tile([FIRST_P, N_STATE // FIRST_P], F32)
+
+        def load_ab(pair):
+            tiles = slice(2 * pair, 2 * pair + 2)
+            nc.sync.dma_start(out=ab_raw[:, tiles, 0:N_STATE], in_=a_rows[:, tiles, :])
+            nc.sync.dma_start(out=ab_raw[:, tiles, N_STATE:N_ALL], in_=b_rows[:, tiles, :])
+
+        def load_v(pair):
+            slots = slice(2 * pair, 2 * pair + 2)
+            nc.sync.dma_start(out=v_raw[:, slots, :], in_=v_rows[:, slots, :])
+
+        def prepare_ab(pair):
+            prepare_pair(nc, banks, ident, ab_raw, pair, ab_grouped, ab_codes, ab_scales)
+
+        def prepare_v(pair):
+            prepare_pair(nc, banks, ident, v_raw, pair, v_grouped, v_codes, v_scales)
+
+        def multiply(pair, h):
+            n_cols = slice(h * N_HALF, (h + 1) * N_HALF)
+            for s in range(2 * pair, 2 * pair + 2):
+                m_cols = slice(s * P, (s + 1) * P)
+                acc = sums.tile([P, N_HALF], F32)
+                for g in range(PASSES):
+                    nc.tensor.matmul_mx(
+                        out=acc[:],
+                        lhsT=v_codes[:, g, m_cols].bitcast(FP8X4),
+                        lhsT_scale=v_scales[:, g, m_cols],
+                        rhs=ab_codes[:, g, n_cols].bitcast(FP8X4),
+                        rhs_scale=ab_scales[:, g, n_cols],
+                        start=(g == 0),
+                        stop=(g == PASSES - 1),
+                    )
+                nc.vector.tensor_tensor(
+                    out=r_sb[:, s, n_cols],
+                    in0=acc[:],
+                    in1=v_raw[:, s + 1, n_cols],
+                    op=mybir.AluOpType.subtract,
+                )
+                nc.sync.dma_start(out=r_next[:, s, n_cols], in_=r_sb[:, s, n_cols])
+
+        with tc.manual_schedule():
+            nc.scalar.dma_start(
+                out=x_first[:], in_=net_input[0:N_STATE].rearrange("(p c) -> p c", p=FIRST_P)
+            )
+            nc.scalar.dma_start(out=x_given[:], in_=x0.rearrange("(p c) -> p c", p=FIRST_P))
+            load_ab(0)
+            load_ab(1)
+            for pair in range(SLOTS // 2):
+                load_v(pair)
+            nc.sync.dma_start(out=v_raw[:, SLOTS, 0:N_STATE], in_=v_next[:, SLOTS - 1, 0:N_STATE])
+            load_ab(2)
+            load_ab(3)
+
+            prepare_ab(0)
+            prepare_ab(1)
+
+            nc.vector.tensor_tensor(
+                out=r_first[:], in0=x_first[:], in1=x_given[:], op=mybir.AluOpType.subtract
+            )
+            nc.sync.dma_start(
+                out=out[0:N_STATE].rearrange("(p c) -> p c", p=FIRST_P), in_=r_first[:]
+            )
+
+            prepare_v(0)
+            for pair in range(SLOTS // 2):
+                if pair + 1 < SLOTS // 2:
+                    prepare_v(pair + 1)
+                else:
+                    prepare_ab(2)
+                    prepare_ab(3)
+                multiply(pair, 0)
+            for pair in range(SLOTS // 2):
+                multiply(pair, 1)

@@ -18,8 +18,7 @@ WORDS = 2
 SLOTS = STEPS // P
 TILES = N_STATE // P
 PAIR = 2 * P
-N_HALF = 512
-HALVES = N_STATE // N_HALF
+PAIRS = SLOTS // 2
 FIRST_P = 16
 
 FLOPS = 2 * STEPS * N_STATE * N_ALL
@@ -91,14 +90,15 @@ def tile_constrainnet_kernel(tc, A, B, x0, net_input, T, out):
         def prepare_v(pair):
             prepare_pair(nc, banks, ident, v_raw, pair, v_grouped, v_codes, v_scales)
 
-        def multiply(pair, h):
-            n_cols = slice(h * N_HALF, (h + 1) * N_HALF)
-            for s in range(2 * pair, 2 * pair + 2):
-                m_cols = slice(s * P, (s + 1) * P)
-                acc = sums.tile([P, N_HALF], F32)
+        def multiply(v_pair, ab_pair):
+            slot = 2 * v_pair
+            n_cols = slice(ab_pair * PAIR, (ab_pair + 1) * PAIR)
+            acc = sums.tile([P, 2, PAIR], F32)
+            for t in range(2):
+                m_cols = slice((slot + t) * P, (slot + t + 1) * P)
                 for g in range(PASSES):
                     nc.tensor.matmul_mx(
-                        out=acc[:],
+                        out=acc[:, t, :],
                         lhsT=v_codes[:, g, m_cols].bitcast(FP8X4),
                         lhsT_scale=v_scales[:, g, m_cols],
                         rhs=ab_codes[:, g, n_cols].bitcast(FP8X4),
@@ -106,13 +106,15 @@ def tile_constrainnet_kernel(tc, A, B, x0, net_input, T, out):
                         start=(g == 0),
                         stop=(g == PASSES - 1),
                     )
-                nc.vector.tensor_tensor(
-                    out=r_sb[:, s, n_cols],
-                    in0=acc[:],
-                    in1=v_raw[:, s + 1, n_cols],
-                    op=mybir.AluOpType.subtract,
-                )
-                nc.sync.dma_start(out=r_next[:, s, n_cols], in_=r_sb[:, s, n_cols])
+            nc.vector.tensor_tensor(
+                out=r_sb[:, slot : slot + 2, n_cols],
+                in0=acc[:],
+                in1=v_raw[:, slot + 1 : slot + 3, n_cols],
+                op=mybir.AluOpType.subtract,
+            )
+            nc.sync.dma_start(
+                out=r_next[:, slot : slot + 2, n_cols], in_=r_sb[:, slot : slot + 2, n_cols]
+            )
 
         with tc.manual_schedule():
             nc.scalar.dma_start(
@@ -120,15 +122,13 @@ def tile_constrainnet_kernel(tc, A, B, x0, net_input, T, out):
             )
             nc.scalar.dma_start(out=x_given[:], in_=x0.rearrange("(p c) -> p c", p=FIRST_P))
             load_ab(0)
-            load_ab(1)
-            for pair in range(SLOTS // 2):
-                load_v(pair)
+            for v_pair in range(PAIRS):
+                load_v(v_pair)
             nc.sync.dma_start(out=v_raw[:, SLOTS, 0:N_STATE], in_=v_next[:, SLOTS - 1, 0:N_STATE])
-            load_ab(2)
-            load_ab(3)
+            for ab_pair in range(1, PAIRS):
+                load_ab(ab_pair)
 
             prepare_ab(0)
-            prepare_ab(1)
 
             nc.vector.tensor_tensor(
                 out=r_first[:], in0=x_first[:], in1=x_given[:], op=mybir.AluOpType.subtract
@@ -138,12 +138,10 @@ def tile_constrainnet_kernel(tc, A, B, x0, net_input, T, out):
             )
 
             prepare_v(0)
-            for pair in range(SLOTS // 2):
-                if pair + 1 < SLOTS // 2:
-                    prepare_v(pair + 1)
-                else:
-                    prepare_ab(2)
-                    prepare_ab(3)
-                multiply(pair, 0)
-            for pair in range(SLOTS // 2):
-                multiply(pair, 1)
+            for ab_pair in range(PAIRS):
+                for v_pair in range(PAIRS):
+                    if ab_pair == 0 and v_pair + 1 < PAIRS:
+                        prepare_v(v_pair + 1)
+                    if v_pair == PAIRS - 1 and ab_pair + 1 < PAIRS:
+                        prepare_ab(ab_pair + 1)
+                    multiply(v_pair, ab_pair)

@@ -18,13 +18,15 @@ WORDS = 2
 SLOTS = STEPS // P
 TILES = N_STATE // P
 PAIR = 2 * P
-PAIRS = SLOTS // 2
+N_HALF = 512
+HALVES = N_STATE // N_HALF
 FIRST_P = 16
+WARM_UP = 4
 
 FLOPS = 2 * STEPS * N_STATE * N_ALL
 
 
-def prepare_pair(nc, banks, ident, raw, pair, grouped, codes, scales):
+def prepare_pair(nc, banks, ident, raw, pair, grouped, codes, scales, hold_clock):
     cols = slice(pair * PAIR, (pair + 1) * PAIR)
     for g in range(PASSES):
         bank = banks.tile([P, WORDS, PAIR], F32)
@@ -35,6 +37,7 @@ def prepare_pair(nc, banks, ident, raw, pair, grouped, codes, scales):
                 nc.tensor.transpose(
                     bank[:, u, t * P : (t + 1) * P], row_words[:, first : first + P], ident[:]
                 )
+        hold_clock()
         nc.scalar.copy(out=grouped[:, g, cols, :], in_=bank[:].rearrange("p u r -> p r u"))
     for g in range(PASSES):
         nc.vector.quantize_mx(
@@ -84,21 +87,30 @@ def tile_constrainnet_kernel(tc, A, B, x0, net_input, T, out):
             slots = slice(2 * pair, 2 * pair + 2)
             nc.sync.dma_start(out=v_raw[:, slots, :], in_=v_rows[:, slots, :])
 
-        def prepare_ab(pair):
-            prepare_pair(nc, banks, ident, ab_raw, pair, ab_grouped, ab_codes, ab_scales)
+        zeros = keep.tile([P, N_HALF], BF16)
+        nc.vector.memset(zeros[:], 0.0)
 
-        def prepare_v(pair):
-            prepare_pair(nc, banks, ident, v_raw, pair, v_grouped, v_codes, v_scales)
+        def matmul_of_zeros():
+            unread = sums.tile([P, N_HALF], F32, tag="acc")
+            nc.tensor.matmul(out=unread[:], lhsT=zeros[:, 0:P], rhs=zeros[:], start=True, stop=True)
 
-        def multiply(v_pair, ab_pair):
-            slot = 2 * v_pair
-            n_cols = slice(ab_pair * PAIR, (ab_pair + 1) * PAIR)
-            acc = sums.tile([P, 2, PAIR], F32)
-            for t in range(2):
-                m_cols = slice((slot + t) * P, (slot + t + 1) * P)
+        def nothing():
+            return None
+
+        def prepare_ab(pair, hold_clock):
+            prepare_pair(nc, banks, ident, ab_raw, pair, ab_grouped, ab_codes, ab_scales, hold_clock)
+
+        def prepare_v(pair, hold_clock):
+            prepare_pair(nc, banks, ident, v_raw, pair, v_grouped, v_codes, v_scales, hold_clock)
+
+        def multiply(pair, h):
+            n_cols = slice(h * N_HALF, (h + 1) * N_HALF)
+            for s in range(2 * pair, 2 * pair + 2):
+                m_cols = slice(s * P, (s + 1) * P)
+                acc = sums.tile([P, N_HALF], F32)
                 for g in range(PASSES):
                     nc.tensor.matmul_mx(
-                        out=acc[:, t, :],
+                        out=acc[:],
                         lhsT=v_codes[:, g, m_cols].bitcast(FP8X4),
                         lhsT_scale=v_scales[:, g, m_cols],
                         rhs=ab_codes[:, g, n_cols].bitcast(FP8X4),
@@ -106,15 +118,13 @@ def tile_constrainnet_kernel(tc, A, B, x0, net_input, T, out):
                         start=(g == 0),
                         stop=(g == PASSES - 1),
                     )
-            nc.vector.tensor_tensor(
-                out=r_sb[:, slot : slot + 2, n_cols],
-                in0=acc[:],
-                in1=v_raw[:, slot + 1 : slot + 3, n_cols],
-                op=mybir.AluOpType.subtract,
-            )
-            nc.sync.dma_start(
-                out=r_next[:, slot : slot + 2, n_cols], in_=r_sb[:, slot : slot + 2, n_cols]
-            )
+                nc.vector.tensor_tensor(
+                    out=r_sb[:, s, n_cols],
+                    in0=acc[:],
+                    in1=v_raw[:, s + 1, n_cols],
+                    op=mybir.AluOpType.subtract,
+                )
+                nc.sync.dma_start(out=r_next[:, s, n_cols], in_=r_sb[:, s, n_cols])
 
         with tc.manual_schedule():
             nc.scalar.dma_start(
@@ -122,13 +132,17 @@ def tile_constrainnet_kernel(tc, A, B, x0, net_input, T, out):
             )
             nc.scalar.dma_start(out=x_given[:], in_=x0.rearrange("(p c) -> p c", p=FIRST_P))
             load_ab(0)
-            for v_pair in range(PAIRS):
-                load_v(v_pair)
+            load_ab(1)
+            for pair in range(SLOTS // 2):
+                load_v(pair)
             nc.sync.dma_start(out=v_raw[:, SLOTS, 0:N_STATE], in_=v_next[:, SLOTS - 1, 0:N_STATE])
-            for ab_pair in range(1, PAIRS):
-                load_ab(ab_pair)
+            load_ab(2)
+            load_ab(3)
 
-            prepare_ab(0)
+            for i in range(WARM_UP):
+                matmul_of_zeros()
+            prepare_ab(0, matmul_of_zeros)
+            prepare_ab(1, matmul_of_zeros)
 
             nc.vector.tensor_tensor(
                 out=r_first[:], in0=x_first[:], in1=x_given[:], op=mybir.AluOpType.subtract
@@ -137,11 +151,15 @@ def tile_constrainnet_kernel(tc, A, B, x0, net_input, T, out):
                 out=out[0:N_STATE].rearrange("(p c) -> p c", p=FIRST_P), in_=r_first[:]
             )
 
-            prepare_v(0)
-            for ab_pair in range(PAIRS):
-                for v_pair in range(PAIRS):
-                    if ab_pair == 0 and v_pair + 1 < PAIRS:
-                        prepare_v(v_pair + 1)
-                    if v_pair == PAIRS - 1 and ab_pair + 1 < PAIRS:
-                        prepare_ab(ab_pair + 1)
-                    multiply(v_pair, ab_pair)
+            prepare_v(0, matmul_of_zeros)
+            prepare_v(1, matmul_of_zeros)
+            multiply(0, 0)
+            for pair in range(1, SLOTS // 2):
+                if pair + 1 < SLOTS // 2:
+                    prepare_v(pair + 1, nothing)
+                else:
+                    prepare_ab(2, nothing)
+                    prepare_ab(3, nothing)
+                multiply(pair, 0)
+            for pair in range(SLOTS // 2):
+                multiply(pair, 1)

from contextlib import ExitStack

import concourse.mybir as mybir
from concourse.masks import make_identity

F32 = mybir.dt.float32
BF16 = mybir.dt.bfloat16
U32 = mybir.dt.uint32
U8 = mybir.dt.uint8
FP8X4 = mybir.dt.float8_e4m3fn_x4

P = 128
N_STATE = 1024
N_ALL = 1536
STEPS = 1024
PASSES = 3
WORDS = 2
SLOTS = STEPS // P
TILES = N_STATE // P
PAIR = 2 * P
N_HALF = 512
HALVES = N_STATE // N_HALF
FIRST_P = 16
WARM_UP = 4

FLOPS = 2 * STEPS * N_STATE * N_ALL


def prepare_pair(nc, banks, ident, raw, pair, grouped, codes, scales, hold_clock):
    cols = slice(pair * PAIR, (pair + 1) * PAIR)
    for g in range(PASSES):
        bank = banks.tile([P, WORDS, PAIR], F32)
        for t in range(2):
            row_words = raw[:, 2 * pair + t, :].bitcast(F32)
            for u in range(WORDS):
                first = (WORDS * g + u) * P
                nc.tensor.transpose(
                    bank[:, u, t * P : (t + 1) * P], row_words[:, first : first + P], ident[:]
                )
        hold_clock()
        nc.scalar.copy(out=grouped[:, g, cols, :], in_=bank[:].rearrange("p u r -> p r u"))
    for g in range(PASSES):
        nc.vector.quantize_mx(
            out=codes[:, g, cols].bitcast(FP8X4),
            scales=scales[:, g, cols],
            in_=grouped[:, g, cols, :].rearrange("p r u -> p (r u)").bitcast(BF16),
        )


def tile_constrainnet_kernel(tc, A, B, x0, net_input, T, out):
    nc = tc.nc
    assert T == STEPS + 1

    v_rows = net_input[0 : STEPS * N_ALL].rearrange("(p s k) -> p s k", s=SLOTS, k=N_ALL)
    v_next = net_input[N_ALL : (STEPS + 1) * N_ALL].rearrange("(p s k) -> p s k", s=SLOTS, k=N_ALL)
    r_next = out[N_STATE : (STEPS + 1) * N_STATE].rearrange("(p s i) -> p s i", s=SLOTS, i=N_STATE)
    a_rows = A.rearrange("(m p) k -> p m k", p=P)
    b_rows = B.rearrange("(m p) k -> p m k", p=P)

    with ExitStack() as ctx:
        keep = ctx.enter_context(tc.tile_pool(name="keep", bufs=1))
        banks = ctx.enter_context(tc.psum_pool(name="banks", bufs=4))
        sums = ctx.enter_context(tc.psum_pool(name="sums", bufs=4))

        ident = keep.tile([P, P], F32)
        make_identity(nc, ident[:])

        ab_raw = keep.tile([P, TILES, N_ALL], BF16)
        v_raw = keep.tile([P, SLOTS + 1, N_ALL], BF16)
        ab_grouped = keep.tile([P, PASSES, N_STATE, WORDS], F32, align_bytes=64)
        v_grouped = keep.tile([P, PASSES, STEPS, WORDS], F32, align_bytes=64)
        ab_codes = keep.tile([P, PASSES, N_STATE], U32, align_bytes=64)
        ab_scales = keep.tile([P, PASSES, N_STATE], U8, align_bytes=64)
        v_codes = keep.tile([P, PASSES, STEPS], U32, align_bytes=64)
        v_scales = keep.tile([P, PASSES, STEPS], U8, align_bytes=64)
        r_sb = keep.tile([P, SLOTS, N_STATE], F32)
        x_first = keep.tile([FIRST_P, N_STATE // FIRST_P], BF16)
        x_given = keep.tile([FIRST_P, N_STATE // FIRST_P], BF16)
        r_first = keep.tile([FIRST_P, N_STATE // FIRST_P], F32)

        def load_ab(pair):
            tiles = slice(2 * pair, 2 * pair + 2)
            nc.sync.dma_start(out=ab_raw[:, tiles, 0:N_STATE], in_=a_rows[:, tiles, :])
            nc.sync.dma_start(out=ab_raw[:, tiles, N_STATE:N_ALL], in_=b_rows[:, tiles, :])

        def load_v(pair):
            slots = slice(2 * pair, 2 * pair + 2)
            nc.sync.dma_start(out=v_raw[:, slots, :], in_=v_rows[:, slots, :])

        zeros = keep.tile([P, N_HALF], BF16)
        nc.vector.memset(zeros[:], 0.0)

        def matmul_of_zeros():
            unread = sums.tile([P, N_HALF], F32, tag="acc")
            nc.tensor.matmul(out=unread[:], lhsT=zeros[:, 0:P], rhs=zeros[:], start=True, stop=True)

        def nothing():
            return None

        def prepare_ab(pair, hold_clock):
            prepare_pair(nc, banks, ident, ab_raw, pair, ab_grouped, ab_codes, ab_scales, hold_clock)

        def prepare_v(pair, hold_clock):
            prepare_pair(nc, banks, ident, v_raw, pair, v_grouped, v_codes, v_scales, hold_clock)

        def multiply(pair, h):
            n_cols = slice(h * N_HALF, (h + 1) * N_HALF)
            for s in range(2 * pair, 2 * pair + 2):
                m_cols = slice(s * P, (s + 1) * P)
                acc = sums.tile([P, N_HALF], F32)
                for g in range(PASSES):
                    nc.tensor.matmul_mx(
                        out=acc[:],
                        lhsT=v_codes[:, g, m_cols].bitcast(FP8X4),
                        lhsT_scale=v_scales[:, g, m_cols],
                        rhs=ab_codes[:, g, n_cols].bitcast(FP8X4),
                        rhs_scale=ab_scales[:, g, n_cols],
                        start=(g == 0),
                        stop=(g == PASSES - 1),
                    )
                nc.vector.tensor_tensor(
                    out=r_sb[:, s, n_cols],
                    in0=acc[:],
                    in1=v_raw[:, s + 1, n_cols],
                    op=mybir.AluOpType.subtract,
                )
                nc.sync.dma_start(out=r_next[:, s, n_cols], in_=r_sb[:, s, n_cols])

        with tc.manual_schedule():
            nc.scalar.dma_start(
                out=x_first[:], in_=net_input[0:N_STATE].rearrange("(p c) -> p c", p=FIRST_P)
            )
            nc.scalar.dma_start(out=x_given[:], in_=x0.rearrange("(p c) -> p c", p=FIRST_P))
            load_ab(0)
            load_ab(1)
            for pair in range(SLOTS // 2):
                load_v(pair)
            nc.sync.dma_start(out=v_raw[:, SLOTS, 0:N_STATE], in_=v_next[:, SLOTS - 1, 0:N_STATE])
            load_ab(2)
            load_ab(3)

            for i in range(WARM_UP):
                matmul_of_zeros()
            prepare_ab(0, matmul_of_zeros)
            prepare_ab(1, matmul_of_zeros)

            nc.vector.tensor_tensor(
                out=r_first[:], in0=x_first[:], in1=x_given[:], op=mybir.AluOpType.subtract
            )
            nc.sync.dma_start(
                out=out[0:N_STATE].rearrange("(p c) -> p c", p=FIRST_P), in_=r_first[:]
            )

            prepare_v(0, matmul_of_zeros)
            prepare_v(1, matmul_of_zeros)
            multiply(0, 0)
            for pair in range(1, SLOTS // 2):
                if pair + 1 < SLOTS // 2:
                    prepare_v(pair + 1, nothing)
                else:
                    prepare_ab(2, nothing)
                    prepare_ab(3, nothing)
                multiply(pair, 0)
            for pair in range(SLOTS // 2):
                multiply(pair, 1)
